import numpy as np
import ml_dtypes


def mxq(x, axis, fmt="e4m3"):
    dtype, down = {"e4m3": (ml_dtypes.float8_e4m3fn, 7), "e5m2": (ml_dtypes.float8_e5m2, 14)}[fmt]
    v = np.moveaxis(np.asarray(x, np.float32).astype(ml_dtypes.bfloat16).astype(np.float64), axis, -1)
    blocks = v.reshape(v.shape[:-1] + (-1, 32))
    amax = np.abs(blocks).max(-1, keepdims=True)
    byte = np.maximum(np.where(amax > 0, np.frexp(amax)[1] - 1 + 127, 0) - down, 1)
    scale = np.exp2(byte - 127.0)
    codes = (blocks / scale).astype(np.float32).astype(dtype).astype(np.float64)
    return np.moveaxis((codes * scale).reshape(v.shape), -1, axis)


WIDE = False


def mx_kscale(k):
    if not WIDE:
        return np.ones(k)
    levels = np.array([10, -10, 5, -5, 0])
    a = np.random.permutation(np.resize(levels, k // 512 * 4)).reshape(k // 512, 4)
    idx = np.arange(k)
    return np.exp2(a[idx // 512, idx % 128 // 32])


BF16 = ml_dtypes.bfloat16


def bf(x):
    return np.asarray(x, np.float32).astype(BF16)


def f64(x):
    return np.asarray(x).astype(np.float64)


B, S, D, H, F = 4, 1024, 1024, 16, 128
EPS = 1e-5
NTERMS = 120


def layernorm(v, gamma, beta):
    mu = v.mean(-1, keepdims=True)
    var = np.square(v - mu).mean(-1, keepdims=True)
    return (v - mu) / np.sqrt(var + EPS) * gamma + beta


def erf(z):
    z = np.clip(z, -6.0, 6.0)
    zz = 2.0 * z * z
    term = z.copy()
    tot = z.copy()
    for n in range(1, NTERMS):
        term *= zz
        term /= 2.0 * n + 1.0
        tot += term
    return 2.0 / np.sqrt(np.pi) * np.exp(-z * z) * tot


def gelu(v):
    return 0.5 * v * (1.0 + erf(v / np.sqrt(2.0)))


def setup_inputs():
    s, t = mx_kscale(D), mx_kscale(D)
    return {"attn_out": bf(0.25 * np.random.standard_normal((B, S, D)) * s),
            "x": bf(np.random.standard_normal((B, S, D)) * (0.5 + np.random.random((B, S, 1))) + 0.5 * np.random.standard_normal((B, S, 1))),
            "w_proj": bf(2.0 * np.random.standard_normal((D, D)) / np.sqrt(D) / s[:, None]),
            "b_proj": bf(0.1 * np.random.standard_normal(D)),
            "g2": bf((1.0 + 0.1 * np.random.standard_normal(D)) * t),
            "beta2": bf(0.1 * np.random.standard_normal(D) * t),
            "w_fc1": bf(np.random.standard_normal((D, F)) / np.sqrt(D) / t[:, None]),
            "b_fc1": bf(0.1 * np.random.standard_normal(F))}


def reference(attn_out, x, w_proj, b_proj, g2, beta2, w_fc1, b_fc1):
    x_mid = f64(x) + ((mxq(f64(attn_out), 2, "e4m3") @ mxq(f64(w_proj), 0, "e4m3")) + f64(b_proj))
    h = layernorm(x_mid, f64(g2), f64(beta2))
    hid = gelu((mxq(h, 2, "e4m3") @ mxq(f64(w_fc1), 0, "e4m3")) + f64(b_fc1))
    return x_mid, hid

@@ -1,0 +1,230 @@
+from contextlib import ExitStack
+
+import concourse.mybir as mybir
+from concourse.masks import make_identity
+
+F32 = mybir.dt.float32
+BF16 = mybir.dt.bfloat16
+U32 = mybir.dt.uint32
+U8 = mybir.dt.uint8
+FP8X4 = mybir.dt.float8_e4m3fn_x4
+ALU = mybir.AluOpType
+ACT = mybir.ActivationFunctionType
+
+P = 128
+PACK = 4
+K_PASS = P * PACK
+TOKENS = 4 * 1024
+D = 1024
+F = 128
+PASSES = D // K_PASS
+BANK = 512
+HALVES = D // BANK
+TILES = TOKENS // P
+GROUP = 4
+EPS = 1e-5
+
+FLOPS = 2 * TOKENS * D * D + 2 * TOKENS * D * F
+
+
+def tile_flashinferblock_pb_t_kernel(
+    tc, attn_out, x, w_proj, b_proj, g2, beta2, w_fc1, b_fc1, out_0, out_1
+):
+    nc = tc.nc
+    attn_view = attn_out.flatten_outer_dims().rearrange("(p i) d -> p i d", i=TILES)
+    x_view = x.flatten_outer_dims().rearrange("(p i) d -> p i d", i=TILES)
+    x_mid_view = out_0.flatten_outer_dims().rearrange("(p i) d -> p i d", i=TILES)
+    hid_view = out_1.flatten_outer_dims().rearrange("(p i) f -> p i f", i=TILES)
+
+    with ExitStack() as ctx:
+        const = ctx.enter_context(tc.tile_pool(name="const", bufs=1))
+        loads = ctx.enter_context(tc.tile_pool(name="loads", bufs=3))
+        work = ctx.enter_context(tc.tile_pool(name="work", bufs=3))
+        stats = ctx.enter_context(tc.tile_pool(name="stats", bufs=4))
+        psum = ctx.enter_context(tc.psum_pool(name="psum", bufs=2))
+
+        w_raw = const.tile([P, PASSES, PACK, D], BF16)
+        for g in range(PASSES):
+            rows = w_proj[g * K_PASS : (g + 1) * K_PASS, :]
+            nc.sync.dma_start(
+                out=w_raw[:, g, :, :].rearrange("q (u e) c -> q u (e c)", e=2),
+                in_=rows.rearrange("(u q e) c -> q u (e c)", u=2, e=2),
+            )
+        w_grouped = const.tile([P, PASSES, D, PACK], BF16, align_bytes=64)
+        w_codes = const.tile([P, PASSES, D], U32, align_bytes=64)
+        w_scales = const.tile([P, PASSES, D], U8, align_bytes=64)
+        for g in range(PASSES):
+            for half in range(HALVES):
+                cols = slice(half * BANK, (half + 1) * BANK)
+                copy = nc.vector.tensor_copy if half == 0 else nc.scalar.copy
+                copy(out=w_grouped[:, g, cols, :], in_=w_raw[:, g, :, cols].rearrange("p t c -> p c t"))
+        for half in range(HALVES):
+            for g in range(PASSES):
+                cols = slice(half * BANK, (half + 1) * BANK)
+                nc.vector.quantize_mx(
+                    out=w_codes[:, g, cols].bitcast(FP8X4),
+                    scales=w_scales[:, g, cols],
+                    in_=w_grouped[:, g, cols, :].rearrange("p c t -> p (c t)"),
+                )
+
+        ident = const.tile([P, P], F32)
+        make_identity(nc, ident[:])
+        neg_half = const.tile([P, 1], F32)
+        nc.vector.memset(neg_half[:], -0.5)
+        b_proj_all = const.tile([P, D], BF16)
+        nc.scalar.dma_start(out=b_proj_all[:], in_=b_proj.partition_broadcast(P))
+        b_fc1_all = const.tile([P, F], BF16)
+        nc.scalar.dma_start(out=b_fc1_all[:], in_=b_fc1.partition_broadcast(P))
+        blocks = D // P
+        norm_rows = const.tile([P, P], BF16)
+        nc.vector.memset(norm_rows[:], 0.0)
+        nc.scalar.dma_start(out=norm_rows[0:blocks, :], in_=g2.rearrange("(c p) -> c p", p=P))
+        nc.scalar.dma_start(out=norm_rows[blocks : 2 * blocks, :], in_=beta2.rearrange("(c p) -> c p", p=P))
+        norm_rows_f32 = const.tile([P, P], F32)
+        nc.vector.tensor_copy(out=norm_rows_f32[:], in_=norm_rows[:])
+        norm_cols_ps = psum.tile([P, PACK, P], F32, tag="z_t")
+        nc.tensor.transpose(norm_cols_ps[:, 0, :], norm_rows_f32[:], ident[:])
+        gain = const.tile([P, blocks], F32)
+        nc.vector.tensor_copy(out=gain[:], in_=norm_cols_ps[:, 0, 0:blocks])
+        shift = const.tile([P, blocks], F32)
+        nc.vector.tensor_copy(out=shift[:], in_=norm_cols_ps[:, 0, blocks : 2 * blocks])
+
+        f_raw = const.tile([P, PASSES, PACK, F], BF16)
+        for g in range(PASSES):
+            rows = w_fc1[g * K_PASS : (g + 1) * K_PASS, :]
+            nc.scalar.dma_start(out=f_raw[:, g, :, :], in_=rows.rearrange("(t p) n -> p t n", p=P))
+        f_grouped = const.tile([P, PASSES, F, PACK], BF16, align_bytes=64)
+        nc.vector.tensor_copy(out=f_grouped[:], in_=f_raw[:].rearrange("p g t n -> p g n t"))
+        f_codes = const.tile([P, PASSES, F], U32, align_bytes=64)
+        f_scales = const.tile([P, PASSES, F], U8, align_bytes=64)
+        nc.vector.quantize_mx(
+            out=f_codes[:].rearrange("p g n -> p (g n)").bitcast(FP8X4),
+            scales=f_scales[:].rearrange("p g n -> p (g n)"),
+            in_=f_grouped[:].rearrange("p g n t -> p (g n t)"),
+        )
+
+        for group in range(TILES // GROUP):
+            tiles = slice(group * GROUP, (group + 1) * GROUP)
+            attn_sb = loads.tile([P, GROUP, D], BF16)
+            nc.sync.dma_start(out=attn_sb[:], in_=attn_view[:, tiles, :])
+            x_sb = loads.tile([P, GROUP, D], BF16)
+            nc.sync.dma_start(out=x_sb[:], in_=x_view[:, tiles, :])
+            hid_ps = psum.tile([P, GROUP, F], F32, bufs=1)
+
+            for j in range(GROUP):
+                attn_words = attn_sb[:, j, :].bitcast(F32)
+                attn_t = psum.tile([P, PASSES * 2, P], F32)
+                for c in range(PASSES * 2):
+                    nc.tensor.transpose(attn_t[:, c, :], attn_words[:, c * P : (c + 1) * P], ident[:])
+                a_grouped = work.tile([P, PASSES, P, PACK], BF16, align_bytes=64)
+                nc.scalar.copy(
+                    out=a_grouped[:].bitcast(F32),
+                    in_=attn_t[:].rearrange("p (g u) r -> p g r u", u=2),
+                )
+                a_codes = work.tile([P, PASSES, P], U32, align_bytes=64)
+                a_scales = work.tile([P, PASSES, P], U8, align_bytes=64)
+                nc.vector.quantize_mx(
+                    out=a_codes[:].rearrange("p g r -> p (g r)").bitcast(FP8X4),
+                    scales=a_scales[:].rearrange("p g r -> p (g r)"),
+                    in_=a_grouped[:].rearrange("p g r t -> p (g r t)"),
+                )
+
+                x_bias = work.tile([P, D], F32)
+                nc.vector.tensor_tensor(out=x_bias[:], in0=x_sb[:, j, :], in1=b_proj_all[:], op=ALU.add)
+                x_mid = work.tile([P, D], F32, bufs=4)
+                row_sums = stats.tile([P, HALVES], F32)
+                for half in range(HALVES):
+                    cols = slice(half * BANK, (half + 1) * BANK)
+                    acc = psum.tile([P, BANK], F32, bufs=3)
+                    for g in range(PASSES):
+                        nc.tensor.matmul_mx(
+                            out=acc[:],
+                            lhsT=a_codes[:, g, :].bitcast(FP8X4),
+                            lhsT_scale=a_scales[:, g, :],
+                            rhs=w_codes[:, g, cols].bitcast(FP8X4),
+                            rhs_scale=w_scales[:, g, cols],
+                            start=(g == 0),
+                            stop=(g == PASSES - 1),
+                        )
+                    nc.vector.scalar_tensor_tensor(
+                        out=x_mid[:, cols],
+                        in0=acc[:],
+                        scalar=1.0,
+                        in1=x_bias[:, cols],
+                        op0=ALU.mult,
+                        op1=ALU.add,
+                        accum_out=row_sums[:, half : half + 1],
+                    )
+                nc.sync.dma_start(out=x_mid_view[:, group * GROUP + j, :], in_=x_mid[:])
+
+                neg_mean = stats.tile([P, 1], F32)
+                nc.vector.tensor_scalar(
+                    out=neg_mean[:],
+                    in0=row_sums[:, 0:1],
+                    scalar1=row_sums[:, 1:2],
+                    scalar2=-1.0 / D,
+                    op0=ALU.add,
+                    op1=ALU.mult,
+                )
+                squares = work.tile([P, D], BF16, bufs=1)
+                sum_squares = stats.tile([P, 1], F32)
+                nc.scalar.activation(
+                    out=squares[:], in_=x_mid[:], func=ACT.Square, bias=neg_mean[:], scale=1.0, accum_out=sum_squares[:]
+                )
+                var_eps = stats.tile([P, 1], F32)
+                nc.gpsimd.tensor_scalar(
+                    out=var_eps[:], in0=sum_squares[:], scalar1=1.0 / D, scalar2=EPS, op0=ALU.mult, op1=ALU.add
+                )
+                inv_std = stats.tile([P, 1], F32)
+                nc.gpsimd.tensor_tensor(out=inv_std[:], in0=var_eps[:], in1=neg_half[:], op=ALU.pow)
+                z = work.tile([P, D], F32)
+                nc.vector.tensor_scalar(
+                    out=z[:], in0=x_mid[:], scalar1=neg_mean[:], scalar2=inv_std[:], op0=ALU.add, op1=ALU.mult
+                )
+
+                h_t = work.tile([P, PASSES, PACK, P], BF16)
+                for g in range(PASSES):
+                    z_t = psum.tile([P, PACK, P], F32)
+                    for t in range(PACK):
+                        c = g * PACK + t
+                        nc.tensor.transpose(z_t[:, t, :], z[:, c * P : (c + 1) * P], ident[:])
+                    for t in range(PACK):
+                        c = g * PACK + t
+                        nc.scalar.activation(
+                            out=h_t[:, g, t, :],
+                            in_=z_t[:, t, :],
+                            func=ACT.Identity,
+                            scale=gain[:, c : c + 1],
+                            bias=shift[:, c : c + 1],
+                        )
+
+                h_grouped = work.tile([P, PASSES, P, PACK], BF16, align_bytes=64)
+                nc.vector.tensor_copy(out=h_grouped[:], in_=h_t[:].rearrange("p g t r -> p g r t"))
+                h_codes = work.tile([P, PASSES, P], U32, align_bytes=64)
+                h_scales = work.tile([P, PASSES, P], U8, align_bytes=64)
+                nc.vector.quantize_mx(
+                    out=h_codes[:].rearrange("p g r -> p (g r)").bitcast(FP8X4),
+                    scales=h_scales[:].rearrange("p g r -> p (g r)"),
+                    in_=h_grouped[:].rearrange("p g r t -> p (g r t)"),
+                )
+                for g in range(PASSES):
+                    nc.tensor.matmul_mx(
+                        out=hid_ps[:, j, :],
+                        lhsT=h_codes[:, g, :].bitcast(FP8X4),
+                        lhsT_scale=h_scales[:, g, :],
+                        rhs=f_codes[:, g, :].bitcast(FP8X4),
+                        rhs_scale=f_scales[:, g, :],
+                        start=(g == 0),
+                        stop=(g == PASSES - 1),
+                    )
+
+            hid_biased = work.tile([P, GROUP, F], F32, bufs=2)
+            nc.vector.tensor_tensor(
+                out=hid_biased[:],
+                in0=hid_ps[:],
+                in1=b_fc1_all[:].unsqueeze(1).to_broadcast([P, GROUP, F]),
+                op=ALU.add,
+            )
+            hid_sb = work.tile([P, GROUP, F], F32, bufs=2)
+            nc.scalar.activation(out=hid_sb[:], in_=hid_biased[:], func=ACT.Gelu)
+            nc.sync.dma_start(out=hid_view[:, tiles, :], in_=hid_sb[:])

@@ -117,7 +117,7 @@ def tile_flashinferblock_pb_t_kernel(
                 for c in range(PASSES * 2):
                     nc.tensor.transpose(attn_t[:, c, :], attn_words[:, c * P : (c + 1) * P], ident[:])
                 a_grouped = work.tile([P, PASSES, P, PACK], BF16, align_bytes=64)
-                nc.scalar.copy(
+                nc.vector.tensor_copy(
                     out=a_grouped[:].bitcast(F32),
                     in_=attn_t[:].rearrange("p (g u) r -> p g r u", u=2),
                 )
@@ -130,8 +130,8 @@ def tile_flashinferblock_pb_t_kernel(
                 )
 
                 x_bias = work.tile([P, D], F32)
-                nc.vector.tensor_tensor(out=x_bias[:], in0=x_sb[:, j, :], in1=b_proj_all[:], op=ALU.add)
-                x_mid = work.tile([P, D], F32, bufs=4)
+                nc.gpsimd.tensor_tensor(out=x_bias[:], in0=x_sb[:, j, :], in1=b_proj_all[:], op=ALU.add)
+                x_mid = work.tile([P, D], F32, bufs=6)
                 row_sums = stats.tile([P, HALVES], F32)
                 for half in range(HALVES):
                     cols = slice(half * BANK, (half + 1) * BANK)
@@ -177,9 +177,11 @@ def tile_flashinferblock_pb_t_kernel(
                 )
                 inv_std = stats.tile([P, 1], F32)
                 nc.gpsimd.tensor_tensor(out=inv_std[:], in0=var_eps[:], in1=neg_half[:], op=ALU.pow)
+                neg_mean_std = stats.tile([P, 1], F32)
+                nc.gpsimd.tensor_tensor(out=neg_mean_std[:], in0=neg_mean[:], in1=inv_std[:], op=ALU.mult)
                 z = work.tile([P, D], F32)
-                nc.vector.tensor_scalar(
-                    out=z[:], in0=x_mid[:], scalar1=neg_mean[:], scalar2=inv_std[:], op0=ALU.add, op1=ALU.mult
+                nc.scalar.activation(
+                    out=z[:], in_=x_mid[:], func=ACT.Identity, scale=inv_std[:], bias=neg_mean_std[:]
                 )
 
                 h_t = work.tile([P, PASSES, PACK, P], BF16)

@@ -20,8 +20,12 @@ F = 128
 PASSES = D // K_PASS
 BANK = 512
 HALVES = D // BANK
+BLOCKS = D // P
 TILES = TOKENS // P
-GROUP = 4
+PAIR = 2
+PAIRS = TILES // PAIR
+STEPS = 9
+AHEAD = 2
 EPS = 1e-5
 
 FLOPS = 2 * TOKENS * D * D + 2 * TOKENS * D * F
@@ -38,26 +42,84 @@ def tile_flashinferblock_pb_t_kernel(
 
     with ExitStack() as ctx:
         const = ctx.enter_context(tc.tile_pool(name="const", bufs=1))
-        loads = ctx.enter_context(tc.tile_pool(name="loads", bufs=3))
+        loads = ctx.enter_context(tc.tile_pool(name="loads", bufs=AHEAD + 2))
         work = ctx.enter_context(tc.tile_pool(name="work", bufs=3))
         stats = ctx.enter_context(tc.tile_pool(name="stats", bufs=4))
         psum = ctx.enter_context(tc.psum_pool(name="psum", bufs=2))
+        ctx.enter_context(tc.manual_schedule())
+
+        attn_sb, x_sb, a_grouped, a_codes, a_scales, x_bias, x_mid = {}, {}, {}, {}, {}, {}, {}
+        neg_mean, inv_std, z, h_t, h_grouped, h_codes, h_scales, hid_biased = {}, {}, {}, {}, {}, {}, {}, {}
+
+        def tiles_of(pair):
+            return slice(pair * PAIR, (pair + 1) * PAIR)
+
+        def load(pair):
+            attn_sb[pair] = loads.tile([P, PAIR, D], BF16, name="attn_sb")
+            nc.sync.dma_start(out=attn_sb[pair][:], in_=attn_view[:, tiles_of(pair), :])
+            x_sb[pair] = loads.tile([P, PAIR, D], BF16, name="x_sb")
+            nc.sync.dma_start(out=x_sb[pair][:], in_=x_view[:, tiles_of(pair), :])
 
         w_raw = const.tile([P, PASSES, PACK, D], BF16)
         for g in range(PASSES):
             rows = w_proj[g * K_PASS : (g + 1) * K_PASS, :]
             nc.sync.dma_start(
-                out=w_raw[:, g, :, :].rearrange("q (u e) c -> q u (e c)", e=2),
-                in_=rows.rearrange("(u q e) c -> q u (e c)", u=2, e=2),
+                out=w_raw[:, g, :, :].rearrange("q (w e) c -> q w (e c)", e=2),
+                in_=rows.rearrange("(w q e) c -> q w (e c)", w=2, e=2),
             )
+        for pair in range(AHEAD):
+            load(pair)
+
+        norm_rows = const.tile([P, P], BF16)
+        nc.vector.memset(norm_rows[:], 0.0)
+        b_proj_all = const.tile([P, D], BF16)
+        nc.scalar.dma_start(out=b_proj_all[:], in_=b_proj.partition_broadcast(P))
+        nc.scalar.dma_start(out=norm_rows[0:BLOCKS, :], in_=g2.rearrange("(c p) -> c p", p=P))
+        nc.scalar.dma_start(out=norm_rows[BLOCKS : 2 * BLOCKS, :], in_=beta2.rearrange("(c p) -> c p", p=P))
+        f_raw = const.tile([P, PASSES, PACK, F], BF16)
+        for g in range(PASSES):
+            rows = w_fc1[g * K_PASS : (g + 1) * K_PASS, :]
+            nc.scalar.dma_start(out=f_raw[:, g, :, :], in_=rows.rearrange("(t p) n -> p t n", p=P))
+        b_fc1_all = const.tile([P, F], BF16)
+        nc.scalar.dma_start(out=b_fc1_all[:], in_=b_fc1.partition_broadcast(P))
+
+        ident = const.tile([P, P], F32)
+        make_identity(nc, ident[:])
+        neg_half = const.tile([P, PAIR], F32)
+        nc.vector.memset(neg_half[:], -0.5)
+
         w_grouped = const.tile([P, PASSES, D, PACK], BF16, align_bytes=64)
         w_codes = const.tile([P, PASSES, D], U32, align_bytes=64)
         w_scales = const.tile([P, PASSES, D], U8, align_bytes=64)
-        for g in range(PASSES):
+
+        def regroup_w(g):
             for half in range(HALVES):
                 cols = slice(half * BANK, (half + 1) * BANK)
                 copy = nc.vector.tensor_copy if half == 0 else nc.scalar.copy
                 copy(out=w_grouped[:, g, cols, :], in_=w_raw[:, g, :, cols].rearrange("p t c -> p c t"))
+
+        regroup_w(0)
+
+        norm_rows_f32 = const.tile([P, P], F32)
+        nc.vector.tensor_copy(out=norm_rows_f32[:], in_=norm_rows[:])
+        norm_cols_ps = psum.tile([P, BANK], F32, tag="z_t")
+        nc.tensor.transpose(norm_cols_ps[:, 0:P], norm_rows_f32[:], ident[:])
+        gain = const.tile([P, BLOCKS], F32)
+        nc.vector.tensor_copy(out=gain[:], in_=norm_cols_ps[:, 0:BLOCKS])
+        shift = const.tile([P, BLOCKS], F32)
+        nc.vector.tensor_copy(out=shift[:], in_=norm_cols_ps[:, BLOCKS : 2 * BLOCKS])
+
+        f_grouped = const.tile([P, PASSES, F, PACK], BF16, align_bytes=64)
+        nc.vector.tensor_copy(out=f_grouped[:], in_=f_raw[:].rearrange("p g t n -> p g n t"))
+        f_codes = const.tile([P, PASSES, F], U32, align_bytes=64)
+        f_scales = const.tile([P, PASSES, F], U8, align_bytes=64)
+
+        regroup_w(1)
+        nc.vector.quantize_mx(
+            out=f_codes[:].rearrange("p g n -> p (g n)").bitcast(FP8X4),
+            scales=f_scales[:].rearrange("p g n -> p (g n)"),
+            in_=f_grouped[:].rearrange("p g n t -> p (g n t)"),
+        )
         for half in range(HALVES):
             for g in range(PASSES):
                 cols = slice(half * BANK, (half + 1) * BANK)
@@ -67,166 +129,170 @@ def tile_flashinferblock_pb_t_kernel(
                     in_=w_grouped[:, g, cols, :].rearrange("p c t -> p (c t)"),
                 )
 
-        ident = const.tile([P, P], F32)
-        make_identity(nc, ident[:])
-        neg_half = const.tile([P, 1], F32)
-        nc.vector.memset(neg_half[:], -0.5)
-        b_proj_all = const.tile([P, D], BF16)
-        nc.scalar.dma_start(out=b_proj_all[:], in_=b_proj.partition_broadcast(P))
-        b_fc1_all = const.tile([P, F], BF16)
-        nc.scalar.dma_start(out=b_fc1_all[:], in_=b_fc1.partition_broadcast(P))
-        blocks = D // P
-        norm_rows = const.tile([P, P], BF16)
-        nc.vector.memset(norm_rows[:], 0.0)
-        nc.scalar.dma_start(out=norm_rows[0:blocks, :], in_=g2.rearrange("(c p) -> c p", p=P))
-        nc.scalar.dma_start(out=norm_rows[blocks : 2 * blocks, :], in_=beta2.rearrange("(c p) -> c p", p=P))
-        norm_rows_f32 = const.tile([P, P], F32)
-        nc.vector.tensor_copy(out=norm_rows_f32[:], in_=norm_rows[:])
-        norm_cols_ps = psum.tile([P, PACK, P], F32, tag="z_t")
-        nc.tensor.transpose(norm_cols_ps[:, 0, :], norm_rows_f32[:], ident[:])
-        gain = const.tile([P, blocks], F32)
-        nc.vector.tensor_copy(out=gain[:], in_=norm_cols_ps[:, 0, 0:blocks])
-        shift = const.tile([P, blocks], F32)
-        nc.vector.tensor_copy(out=shift[:], in_=norm_cols_ps[:, 0, blocks : 2 * blocks])
-
-        f_raw = const.tile([P, PASSES, PACK, F], BF16)
-        for g in range(PASSES):
-            rows = w_fc1[g * K_PASS : (g + 1) * K_PASS, :]
-            nc.scalar.dma_start(out=f_raw[:, g, :, :], in_=rows.rearrange("(t p) n -> p t n", p=P))
-        f_grouped = const.tile([P, PASSES, F, PACK], BF16, align_bytes=64)
-        nc.vector.tensor_copy(out=f_grouped[:], in_=f_raw[:].rearrange("p g t n -> p g n t"))
-        f_codes = const.tile([P, PASSES, F], U32, align_bytes=64)
-        f_scales = const.tile([P, PASSES, F], U8, align_bytes=64)
-        nc.vector.quantize_mx(
-            out=f_codes[:].rearrange("p g n -> p (g n)").bitcast(FP8X4),
-            scales=f_scales[:].rearrange("p g n -> p (g n)"),
-            in_=f_grouped[:].rearrange("p g n t -> p (g n t)"),
-        )
-
-        for group in range(TILES // GROUP):
-            tiles = slice(group * GROUP, (group + 1) * GROUP)
-            attn_sb = loads.tile([P, GROUP, D], BF16)
-            nc.sync.dma_start(out=attn_sb[:], in_=attn_view[:, tiles, :])
-            x_sb = loads.tile([P, GROUP, D], BF16)
-            nc.sync.dma_start(out=x_sb[:], in_=x_view[:, tiles, :])
-            hid_ps = psum.tile([P, GROUP, F], F32, bufs=1)
-
-            for j in range(GROUP):
-                attn_words = attn_sb[:, j, :].bitcast(F32)
+        def transpose_attn(pair):
+            a_grouped[pair] = work.tile([P, PASSES, PAIR, P, PACK], BF16, name="a_grouped", align_bytes=64)
+            a_words = a_grouped[pair][:].bitcast(F32)
+            for j in range(PAIR):
+                attn_words = attn_sb[pair][:, j, :].bitcast(F32)
                 attn_t = psum.tile([P, PASSES * 2, P], F32)
                 for c in range(PASSES * 2):
                     nc.tensor.transpose(attn_t[:, c, :], attn_words[:, c * P : (c + 1) * P], ident[:])
-                a_grouped = work.tile([P, PASSES, P, PACK], BF16, align_bytes=64)
-                nc.vector.tensor_copy(
-                    out=a_grouped[:].bitcast(F32),
-                    in_=attn_t[:].rearrange("p (g u) r -> p g r u", u=2),
-                )
-                a_codes = work.tile([P, PASSES, P], U32, align_bytes=64)
-                a_scales = work.tile([P, PASSES, P], U8, align_bytes=64)
-                nc.vector.quantize_mx(
-                    out=a_codes[:].rearrange("p g r -> p (g r)").bitcast(FP8X4),
-                    scales=a_scales[:].rearrange("p g r -> p (g r)"),
-                    in_=a_grouped[:].rearrange("p g r t -> p (g r t)"),
-                )
+                nc.scalar.copy(out=a_words[:, :, j, :, :], in_=attn_t[:].rearrange("p (g w) r -> p g r w", w=2))
 
-                x_bias = work.tile([P, D], F32)
-                nc.gpsimd.tensor_tensor(out=x_bias[:], in0=x_sb[:, j, :], in1=b_proj_all[:], op=ALU.add)
-                x_mid = work.tile([P, D], F32, bufs=6)
-                row_sums = stats.tile([P, HALVES], F32)
+        def quantise_attn(pair):
+            a_codes[pair] = work.tile([P, PASSES, PAIR, P], U32, name="a_codes", align_bytes=64)
+            a_scales[pair] = work.tile([P, PASSES, PAIR, P], U8, name="a_scales", align_bytes=64)
+            nc.vector.quantize_mx(
+                out=a_codes[pair][:].rearrange("p g j r -> p (g j r)").bitcast(FP8X4),
+                scales=a_scales[pair][:].rearrange("p g j r -> p (g j r)"),
+                in_=a_grouped[pair][:].rearrange("p g j r t -> p (g j r t)"),
+            )
+
+        def add_bias(pair):
+            x_bias[pair] = work.tile([P, PAIR, D], F32, name="x_bias", bufs=2)
+            nc.vector.tensor_tensor(
+                out=x_bias[pair][:],
+                in0=x_sb[pair][:],
+                in1=b_proj_all[:].unsqueeze(1).to_broadcast([P, PAIR, D]),
+                op=ALU.add,
+            )
+
+        def project(pair):
+            x_mid[pair] = work.tile([P, PAIR, D], F32, name="x_mid", bufs=4)
+            half_sums = stats.tile([P, PAIR, HALVES], F32)
+            for j in range(PAIR):
                 for half in range(HALVES):
                     cols = slice(half * BANK, (half + 1) * BANK)
                     acc = psum.tile([P, BANK], F32, bufs=3)
                     for g in range(PASSES):
                         nc.tensor.matmul_mx(
                             out=acc[:],
-                            lhsT=a_codes[:, g, :].bitcast(FP8X4),
-                            lhsT_scale=a_scales[:, g, :],
+                            lhsT=a_codes[pair][:, g, j, :].bitcast(FP8X4),
+                            lhsT_scale=a_scales[pair][:, g, j, :],
                             rhs=w_codes[:, g, cols].bitcast(FP8X4),
                             rhs_scale=w_scales[:, g, cols],
                             start=(g == 0),
                             stop=(g == PASSES - 1),
                         )
                     nc.vector.scalar_tensor_tensor(
-                        out=x_mid[:, cols],
+                        out=x_mid[pair][:, j, cols],
                         in0=acc[:],
                         scalar=1.0,
-                        in1=x_bias[:, cols],
+                        in1=x_bias[pair][:, j, cols],
                         op0=ALU.mult,
                         op1=ALU.add,
-                        accum_out=row_sums[:, half : half + 1],
+                        accum_out=half_sums[:, j, half : half + 1],
                     )
-                nc.sync.dma_start(out=x_mid_view[:, group * GROUP + j, :], in_=x_mid[:])
+            nc.sync.dma_start(out=x_mid_view[:, tiles_of(pair), :], in_=x_mid[pair][:])
+            row_sums = stats.tile([P, PAIR], F32)
+            nc.gpsimd.tensor_tensor(out=row_sums[:], in0=half_sums[:, :, 0], in1=half_sums[:, :, 1], op=ALU.add)
+            neg_mean[pair] = stats.tile([P, PAIR], F32, name="neg_mean")
+            nc.gpsimd.tensor_scalar(
+                out=neg_mean[pair][:], in0=row_sums[:], scalar1=-1.0 / D, scalar2=0.0, op0=ALU.mult, op1=ALU.add
+            )
 
-                neg_mean = stats.tile([P, 1], F32)
+        def variance(pair):
+            sum_squares = stats.tile([P, PAIR], F32)
+            for j in range(PAIR):
+                squares = work.tile([P, D], BF16, bufs=1)
+                nc.scalar.activation(
+                    out=squares[:],
+                    in_=x_mid[pair][:, j, :],
+                    func=ACT.Square,
+                    bias=neg_mean[pair][:, j : j + 1],
+                    scale=1.0,
+                    accum_out=sum_squares[:, j : j + 1],
+                )
+            var_eps = stats.tile([P, PAIR], F32)
+            nc.gpsimd.tensor_scalar(
+                out=var_eps[:], in0=sum_squares[:], scalar1=1.0 / D, scalar2=EPS, op0=ALU.mult, op1=ALU.add
+            )
+            inv_std[pair] = stats.tile([P, PAIR], F32, name="inv_std")
+            nc.gpsimd.tensor_tensor(out=inv_std[pair][:], in0=var_eps[:], in1=neg_half[:], op=ALU.pow)
+
+        def normalise(pair):
+            z[pair] = work.tile([P, PAIR, D], F32, name="z")
+            for j in range(PAIR):
                 nc.vector.tensor_scalar(
-                    out=neg_mean[:],
-                    in0=row_sums[:, 0:1],
-                    scalar1=row_sums[:, 1:2],
-                    scalar2=-1.0 / D,
+                    out=z[pair][:, j, :],
+                    in0=x_mid[pair][:, j, :],
+                    scalar1=neg_mean[pair][:, j : j + 1],
+                    scalar2=inv_std[pair][:, j : j + 1],
                     op0=ALU.add,
                     op1=ALU.mult,
                 )
-                squares = work.tile([P, D], BF16, bufs=1)
-                sum_squares = stats.tile([P, 1], F32)
-                nc.scalar.activation(
-                    out=squares[:], in_=x_mid[:], func=ACT.Square, bias=neg_mean[:], scale=1.0, accum_out=sum_squares[:]
-                )
-                var_eps = stats.tile([P, 1], F32)
-                nc.gpsimd.tensor_scalar(
-                    out=var_eps[:], in0=sum_squares[:], scalar1=1.0 / D, scalar2=EPS, op0=ALU.mult, op1=ALU.add
-                )
-                inv_std = stats.tile([P, 1], F32)
-                nc.gpsimd.tensor_tensor(out=inv_std[:], in0=var_eps[:], in1=neg_half[:], op=ALU.pow)
-                neg_mean_std = stats.tile([P, 1], F32)
-                nc.gpsimd.tensor_tensor(out=neg_mean_std[:], in0=neg_mean[:], in1=inv_std[:], op=ALU.mult)
-                z = work.tile([P, D], F32)
-                nc.scalar.activation(
-                    out=z[:], in_=x_mid[:], func=ACT.Identity, scale=inv_std[:], bias=neg_mean_std[:]
-                )
 
-                h_t = work.tile([P, PASSES, PACK, P], BF16)
-                for g in range(PASSES):
-                    z_t = psum.tile([P, PACK, P], F32)
-                    for t in range(PACK):
-                        c = g * PACK + t
-                        nc.tensor.transpose(z_t[:, t, :], z[:, c * P : (c + 1) * P], ident[:])
-                    for t in range(PACK):
-                        c = g * PACK + t
-                        nc.scalar.activation(
-                            out=h_t[:, g, t, :],
-                            in_=z_t[:, t, :],
-                            func=ACT.Identity,
-                            scale=gain[:, c : c + 1],
-                            bias=shift[:, c : c + 1],
-                        )
+        def regroup_h(copy, pair, g):
+            planes = h_t[pair][:, g * PACK : (g + 1) * PACK, :, :]
+            copy(out=h_grouped[pair][:, g, :, :], in_=planes.rearrange("p t j r -> p (j r) t"))
 
-                h_grouped = work.tile([P, PASSES, P, PACK], BF16, align_bytes=64)
-                nc.vector.tensor_copy(out=h_grouped[:], in_=h_t[:].rearrange("p g t r -> p g r t"))
-                h_codes = work.tile([P, PASSES, P], U32, align_bytes=64)
-                h_scales = work.tile([P, PASSES, P], U8, align_bytes=64)
-                nc.vector.quantize_mx(
-                    out=h_codes[:].rearrange("p g r -> p (g r)").bitcast(FP8X4),
-                    scales=h_scales[:].rearrange("p g r -> p (g r)"),
-                    in_=h_grouped[:].rearrange("p g r t -> p (g r t)"),
-                )
+        def transpose_norm(pair):
+            h_t[pair] = work.tile([P, BLOCKS, PAIR, P], BF16, name="h_t")
+            h_grouped[pair] = work.tile([P, PASSES, PAIR * P, PACK], BF16, name="h_grouped", align_bytes=64)
+            for first in range(0, BLOCKS, 2):
+                z_t = psum.tile([P, 2, PAIR, P], F32)
+                for c in range(first, first + 2):
+                    for j in range(PAIR):
+                        nc.tensor.transpose(z_t[:, c - first, j, :], z[pair][:, j, c * P : (c + 1) * P], ident[:])
+                for c in range(first, first + 2):
+                    nc.scalar.activation(
+                        out=h_t[pair][:, c, :, :],
+                        in_=z_t[:, c - first, :, :],
+                        func=ACT.Identity,
+                        scale=gain[:, c : c + 1],
+                        bias=shift[:, c : c + 1],
+                    )
+            regroup_h(nc.scalar.copy, pair, 1)
+
+        def quantise_h(pair):
+            h_codes[pair] = work.tile([P, PASSES, PAIR, P], U32, name="h_codes", align_bytes=64)
+            h_scales[pair] = work.tile([P, PASSES, PAIR, P], U8, name="h_scales", align_bytes=64)
+            nc.vector.quantize_mx(
+                out=h_codes[pair][:].rearrange("p g j r -> p (g j r)").bitcast(FP8X4),
+                scales=h_scales[pair][:].rearrange("p g j r -> p (g j r)"),
+                in_=h_grouped[pair][:].rearrange("p g r t -> p (g r t)"),
+            )
+
+        def second_product(pair):
+            hid_ps = psum.tile([P, PAIR, F], F32, bufs=1)
+            for j in range(PAIR):
                 for g in range(PASSES):
                     nc.tensor.matmul_mx(
                         out=hid_ps[:, j, :],
-                        lhsT=h_codes[:, g, :].bitcast(FP8X4),
-                        lhsT_scale=h_scales[:, g, :],
+                        lhsT=h_codes[pair][:, g, j, :].bitcast(FP8X4),
+                        lhsT_scale=h_scales[pair][:, g, j, :],
                         rhs=f_codes[:, g, :].bitcast(FP8X4),
                         rhs_scale=f_scales[:, g, :],
                         start=(g == 0),
                         stop=(g == PASSES - 1),
                     )
-
-            hid_biased = work.tile([P, GROUP, F], F32, bufs=2)
+            hid_biased[pair] = work.tile([P, PAIR, F], F32, name="hid_biased")
             nc.vector.tensor_tensor(
-                out=hid_biased[:],
+                out=hid_biased[pair][:],
                 in0=hid_ps[:],
-                in1=b_fc1_all[:].unsqueeze(1).to_broadcast([P, GROUP, F]),
+                in1=b_fc1_all[:].unsqueeze(1).to_broadcast([P, PAIR, F]),
                 op=ALU.add,
             )
-            hid_sb = work.tile([P, GROUP, F], F32, bufs=2)
-            nc.scalar.activation(out=hid_sb[:], in_=hid_biased[:], func=ACT.Gelu)
-            nc.sync.dma_start(out=hid_view[:, tiles, :], in_=hid_sb[:])
+
+        def finish(pair):
+            hid_sb = work.tile([P, PAIR, F], F32)
+            nc.scalar.activation(out=hid_sb[:], in_=hid_biased[pair][:], func=ACT.Gelu)
+            nc.sync.dma_start(out=hid_view[:, tiles_of(pair), :], in_=hid_sb[:])
+
+        def step(function, pair):
+            if 0 <= pair < PAIRS:
+                function(pair)
+
+        for m in range(PAIRS + STEPS - 1):
+            step(load, m + AHEAD)
+            step(project, m - 2)
+            step(finish, m - 8)
+            step(variance, m - 3)
+            step(lambda pair: regroup_h(nc.vector.tensor_copy, pair, 0), m - 6)
+            step(quantise_attn, m - 1)
+            step(add_bias, m - 1)
+            step(transpose_norm, m - 5)
+            step(quantise_h, m - 6)
+            step(normalise, m - 4)
+            step(transpose_attn, m)
+            step(second_product, m - 7)

@@ -49,7 +49,7 @@ def tile_flashinferblock_pb_t_kernel(
         ctx.enter_context(tc.manual_schedule())
 
         attn_sb, x_sb, a_grouped, a_codes, a_scales, x_bias, x_mid = {}, {}, {}, {}, {}, {}, {}
-        neg_mean, inv_std, z, h_t, h_grouped, h_codes, h_scales, hid_biased = {}, {}, {}, {}, {}, {}, {}, {}
+        half_sums, neg_mean, inv_std, z, h_t, h_grouped, h_codes, h_scales, hid_biased = {}, {}, {}, {}, {}, {}, {}, {}, {}
 
         def tiles_of(pair):
             return slice(pair * PAIR, (pair + 1) * PAIR)
@@ -159,7 +159,7 @@ def tile_flashinferblock_pb_t_kernel(
 
         def project(pair):
             x_mid[pair] = work.tile([P, PAIR, D], F32, name="x_mid", bufs=4)
-            half_sums = stats.tile([P, PAIR, HALVES], F32)
+            half_sums[pair] = stats.tile([P, PAIR, HALVES], F32, name="half_sums")
             for j in range(PAIR):
                 for half in range(HALVES):
                     cols = slice(half * BANK, (half + 1) * BANK)
@@ -181,19 +181,22 @@ def tile_flashinferblock_pb_t_kernel(
                         in1=x_bias[pair][:, j, cols],
                         op0=ALU.mult,
                         op1=ALU.add,
-                        accum_out=half_sums[:, j, half : half + 1],
+                        accum_out=half_sums[pair][:, j, half : half + 1],
                     )
             nc.sync.dma_start(out=x_mid_view[:, tiles_of(pair), :], in_=x_mid[pair][:])
-            row_sums = stats.tile([P, PAIR], F32)
-            nc.gpsimd.tensor_tensor(out=row_sums[:], in0=half_sums[:, :, 0], in1=half_sums[:, :, 1], op=ALU.add)
-            neg_mean[pair] = stats.tile([P, PAIR], F32, name="neg_mean")
-            nc.gpsimd.tensor_scalar(
-                out=neg_mean[pair][:], in0=row_sums[:], scalar1=-1.0 / D, scalar2=0.0, op0=ALU.mult, op1=ALU.add
-            )
 
         def variance(pair):
+            neg_mean[pair] = stats.tile([P, PAIR], F32, name="neg_mean")
             sum_squares = stats.tile([P, PAIR], F32)
             for j in range(PAIR):
+                scaled_sums = stats.tile([P, HALVES], F32)
+                nc.scalar.activation(
+                    out=scaled_sums[:],
+                    in_=half_sums[pair][:, j, :],
+                    func=ACT.Copy,
+                    scale=-1.0 / D,
+                    accum_out=neg_mean[pair][:, j : j + 1],
+                )
                 squares = work.tile([P, D], BF16, bufs=1)
                 nc.scalar.activation(
                     out=squares[:],
@@ -213,7 +216,7 @@ def tile_flashinferblock_pb_t_kernel(
         def normalise(pair):
             z[pair] = work.tile([P, PAIR, D], F32, name="z")
             for j in range(PAIR):
-                nc.vector.tensor_scalar(
+                nc.gpsimd.tensor_scalar(
                     out=z[pair][:, j, :],
                     in0=x_mid[pair][:, j, :],
                     scalar1=neg_mean[pair][:, j : j + 1],
@@ -222,9 +225,16 @@ def tile_flashinferblock_pb_t_kernel(
                     op1=ALU.mult,
                 )
 
-        def regroup_h(copy, pair, g):
-            planes = h_t[pair][:, g * PACK : (g + 1) * PACK, :, :]
-            copy(out=h_grouped[pair][:, g, :, :], in_=planes.rearrange("p t j r -> p (j r) t"))
+        def regroup_h(copy, pair, g, tokens):
+            planes = h_t[pair][:, g * PACK : (g + 1) * PACK, :, :].rearrange("p t j r -> p t (j r)")
+            copy(
+                out=h_grouped[pair][:, g, tokens, :].rearrange("p (c i) t -> p c t i", i=4),
+                in_=planes[:, :, tokens].rearrange("p t (c i) -> p c t i", i=4),
+            )
+
+        def regroup_h_vector(pair):
+            regroup_h(nc.vector.tensor_copy, pair, 0, slice(0, PAIR * P))
+            regroup_h(nc.vector.tensor_copy, pair, 1, slice(0, P))
 
         def transpose_norm(pair):
             h_t[pair] = work.tile([P, BLOCKS, PAIR, P], BF16, name="h_t")
@@ -242,7 +252,7 @@ def tile_flashinferblock_pb_t_kernel(
                         scale=gain[:, c : c + 1],
                         bias=shift[:, c : c + 1],
                     )
-            regroup_h(nc.scalar.copy, pair, 1)
+            regroup_h(nc.scalar.copy, pair, 1, slice(P, PAIR * P))
 
         def quantise_h(pair):
             h_codes[pair] = work.tile([P, PASSES, PAIR, P], U32, name="h_codes", align_bytes=64)
@@ -288,11 +298,11 @@ def tile_flashinferblock_pb_t_kernel(
             step(project, m - 2)
             step(finish, m - 8)
             step(variance, m - 3)
-            step(lambda pair: regroup_h(nc.vector.tensor_copy, pair, 0), m - 6)
+            step(normalise, m - 3)
+            step(regroup_h_vector, m - 6)
             step(quantise_attn, m - 1)
             step(add_bias, m - 1)
             step(transpose_norm, m - 5)
             step(quantise_h, m - 6)
-            step(normalise, m - 4)
             step(transpose_attn, m)
             step(second_product, m - 7)

@@ -19,9 +19,11 @@ D = 1024
 F = 128
 PASSES = D // K_PASS
 BANK = 512
+BANKS = 8
 HALVES = D // BANK
 BLOCKS = D // P
 TILES = TOKENS // P
+RUN = 4
 PAIR = 2
 PAIRS = TILES // PAIR
 STEPS = 9
@@ -45,11 +47,20 @@ def tile_flashinferblock_pb_t_kernel(
         loads = ctx.enter_context(tc.tile_pool(name="loads", bufs=AHEAD + 2))
         work = ctx.enter_context(tc.tile_pool(name="work", bufs=3))
         stats = ctx.enter_context(tc.tile_pool(name="stats", bufs=4))
-        psum = ctx.enter_context(tc.psum_pool(name="psum", bufs=2))
+        psum = ctx.enter_context(tc.psum_pool(name="psum", bufs=BANKS))
         ctx.enter_context(tc.manual_schedule())
 
         attn_sb, x_sb, a_grouped, a_codes, a_scales, x_bias, x_mid = {}, {}, {}, {}, {}, {}, {}
         half_sums, neg_mean, inv_std, z, h_t, h_grouped, h_codes, h_scales, hid_biased = {}, {}, {}, {}, {}, {}, {}, {}, {}
+
+        def bank(shape):
+            return psum.tile(shape, F32, name="bank")
+
+        def regroup(copy, grouped, planes):
+            copy(
+                out=grouped.rearrange("p (c i) t -> p c t i", i=RUN),
+                in_=planes.rearrange("p t (c i) -> p c t i", i=RUN),
+            )
 
         def tiles_of(pair):
             return slice(pair * PAIR, (pair + 1) * PAIR)
@@ -96,13 +107,13 @@ def tile_flashinferblock_pb_t_kernel(
             for half in range(HALVES):
                 cols = slice(half * BANK, (half + 1) * BANK)
                 copy = nc.vector.tensor_copy if half == 0 else nc.scalar.copy
-                copy(out=w_grouped[:, g, cols, :], in_=w_raw[:, g, :, cols].rearrange("p t c -> p c t"))
+                regroup(copy, w_grouped[:, g, cols, :], w_raw[:, g, :, cols])
 
         regroup_w(0)
 
         norm_rows_f32 = const.tile([P, P], F32)
         nc.vector.tensor_copy(out=norm_rows_f32[:], in_=norm_rows[:])
-        norm_cols_ps = psum.tile([P, BANK], F32, tag="z_t")
+        norm_cols_ps = bank([P, BANK])
         nc.tensor.transpose(norm_cols_ps[:, 0:P], norm_rows_f32[:], ident[:])
         gain = const.tile([P, BLOCKS], F32)
         nc.vector.tensor_copy(out=gain[:], in_=norm_cols_ps[:, 0:BLOCKS])
@@ -110,7 +121,8 @@ def tile_flashinferblock_pb_t_kernel(
         nc.vector.tensor_copy(out=shift[:], in_=norm_cols_ps[:, BLOCKS : 2 * BLOCKS])
 
         f_grouped = const.tile([P, PASSES, F, PACK], BF16, align_bytes=64)
-        nc.vector.tensor_copy(out=f_grouped[:], in_=f_raw[:].rearrange("p g t n -> p g n t"))
+        for g in range(PASSES):
+            regroup(nc.vector.tensor_copy, f_grouped[:, g, :, :], f_raw[:, g, :, :])
         f_codes = const.tile([P, PASSES, F], U32, align_bytes=64)
         f_scales = const.tile([P, PASSES, F], U8, align_bytes=64)
 
@@ -134,7 +146,7 @@ def tile_flashinferblock_pb_t_kernel(
             a_words = a_grouped[pair][:].bitcast(F32)
             for j in range(PAIR):
                 attn_words = attn_sb[pair][:, j, :].bitcast(F32)
-                attn_t = psum.tile([P, PASSES * 2, P], F32)
+                attn_t = bank([P, PASSES * 2, P])
                 for c in range(PASSES * 2):
                     nc.tensor.transpose(attn_t[:, c, :], attn_words[:, c * P : (c + 1) * P], ident[:])
                 nc.scalar.copy(out=a_words[:, :, j, :, :], in_=attn_t[:].rearrange("p (g w) r -> p g r w", w=2))
@@ -163,7 +175,7 @@ def tile_flashinferblock_pb_t_kernel(
             for j in range(PAIR):
                 for half in range(HALVES):
                     cols = slice(half * BANK, (half + 1) * BANK)
-                    acc = psum.tile([P, BANK], F32, bufs=3)
+                    acc = bank([P, BANK])
                     for g in range(PASSES):
                         nc.tensor.matmul_mx(
                             out=acc[:],
@@ -227,10 +239,7 @@ def tile_flashinferblock_pb_t_kernel(
 
         def regroup_h(copy, pair, g, tokens):
             planes = h_t[pair][:, g * PACK : (g + 1) * PACK, :, :].rearrange("p t j r -> p t (j r)")
-            copy(
-                out=h_grouped[pair][:, g, tokens, :].rearrange("p (c i) t -> p c t i", i=4),
-                in_=planes[:, :, tokens].rearrange("p t (c i) -> p c t i", i=4),
-            )
+            regroup(copy, h_grouped[pair][:, g, tokens, :], planes[:, :, tokens])
 
         def regroup_h_vector(pair):
             regroup_h(nc.vector.tensor_copy, pair, 0, slice(0, PAIR * P))
@@ -240,7 +249,7 @@ def tile_flashinferblock_pb_t_kernel(
             h_t[pair] = work.tile([P, BLOCKS, PAIR, P], BF16, name="h_t")
             h_grouped[pair] = work.tile([P, PASSES, PAIR * P, PACK], BF16, name="h_grouped", align_bytes=64)
             for first in range(0, BLOCKS, 2):
-                z_t = psum.tile([P, 2, PAIR, P], F32)
+                z_t = bank([P, 2, PAIR, P])
                 for c in range(first, first + 2):
                     for j in range(PAIR):
                         nc.tensor.transpose(z_t[:, c - first, j, :], z[pair][:, j, c * P : (c + 1) * P], ident[:])
@@ -264,7 +273,7 @@ def tile_flashinferblock_pb_t_kernel(
             )
 
         def second_product(pair):
-            hid_ps = psum.tile([P, PAIR, F], F32, bufs=1)
+            hid_ps = bank([P, PAIR, F])
             for j in range(PAIR):
                 for g in range(PASSES):
                     nc.tensor.matmul_mx(

@@ -47,7 +47,8 @@ def tile_flashinferblock_pb_t_kernel(
         loads = ctx.enter_context(tc.tile_pool(name="loads", bufs=AHEAD + 2))
         work = ctx.enter_context(tc.tile_pool(name="work", bufs=3))
         stats = ctx.enter_context(tc.tile_pool(name="stats", bufs=4))
-        psum = ctx.enter_context(tc.psum_pool(name="psum", bufs=BANKS))
+        psum_const = ctx.enter_context(tc.psum_pool(name="psum_const", bufs=1))
+        psum = ctx.enter_context(tc.psum_pool(name="psum", bufs=BANKS - HALVES))
         ctx.enter_context(tc.manual_schedule())
 
         attn_sb, x_sb, a_grouped, a_codes, a_scales, x_bias, x_mid = {}, {}, {}, {}, {}, {}, {}
@@ -83,8 +84,11 @@ def tile_flashinferblock_pb_t_kernel(
 
         norm_rows = const.tile([P, P], BF16)
         nc.vector.memset(norm_rows[:], 0.0)
-        b_proj_all = const.tile([P, D], BF16)
-        nc.scalar.dma_start(out=b_proj_all[:], in_=b_proj.partition_broadcast(P))
+        b_proj_row = const.tile([P, D], BF16)
+        nc.vector.memset(b_proj_row[:], 0.0)
+        ones = const.tile([P, P], BF16)
+        nc.vector.memset(ones[:], 1.0)
+        nc.scalar.dma_start(out=b_proj_row[0:1, :], in_=b_proj.rearrange("(o d) -> o d", o=1))
         nc.scalar.dma_start(out=norm_rows[0:BLOCKS, :], in_=g2.rearrange("(c p) -> c p", p=P))
         nc.scalar.dma_start(out=norm_rows[BLOCKS : 2 * BLOCKS, :], in_=beta2.rearrange("(c p) -> c p", p=P))
         f_raw = const.tile([P, PASSES, PACK, F], BF16)
@@ -110,6 +114,17 @@ def tile_flashinferblock_pb_t_kernel(
                 regroup(copy, w_grouped[:, g, cols, :], w_raw[:, g, :, cols])
 
         regroup_w(0)
+
+        b_proj_all = []
+        for half in range(HALVES):
+            b_proj_all.append(psum_const.tile([P, BANK], F32, name="b_proj_all%d" % half))
+            nc.tensor.matmul(
+                out=b_proj_all[half][:],
+                lhsT=ones[:],
+                rhs=b_proj_row[:, half * BANK : (half + 1) * BANK],
+                start=True,
+                stop=True,
+            )
 
         norm_rows_f32 = const.tile([P, P], F32)
         nc.vector.tensor_copy(out=norm_rows_f32[:], in_=norm_rows[:])
@@ -162,12 +177,14 @@ def tile_flashinferblock_pb_t_kernel(
 
         def add_bias(pair):
             x_bias[pair] = work.tile([P, PAIR, D], F32, name="x_bias", bufs=2)
-            nc.vector.tensor_tensor(
-                out=x_bias[pair][:],
-                in0=x_sb[pair][:],
-                in1=b_proj_all[:].unsqueeze(1).to_broadcast([P, PAIR, D]),
-                op=ALU.add,
-            )
+            for half in range(HALVES):
+                cols = slice(half * BANK, (half + 1) * BANK)
+                nc.vector.tensor_tensor(
+                    out=x_bias[pair][:, :, cols],
+                    in0=b_proj_all[half][:].unsqueeze(1).to_broadcast([P, PAIR, BANK]),
+                    in1=x_sb[pair][:, :, cols],
+                    op=ALU.add,
+                )
 
         def project(pair):
             x_mid[pair] = work.tile([P, PAIR, D], F32, name="x_mid", bufs=4)
@@ -310,8 +327,8 @@ def tile_flashinferblock_pb_t_kernel(
             step(normalise, m - 3)
             step(regroup_h_vector, m - 6)
             step(quantise_attn, m - 1)
-            step(add_bias, m - 1)
             step(transpose_norm, m - 5)
             step(quantise_h, m - 6)
+            step(add_bias, m - 1)
             step(transpose_attn, m)
             step(second_product, m - 7)

from contextlib import ExitStack

import concourse.mybir as mybir
from concourse.masks import make_identity

F32 = mybir.dt.float32
BF16 = mybir.dt.bfloat16
U32 = mybir.dt.uint32
U8 = mybir.dt.uint8
FP8X4 = mybir.dt.float8_e4m3fn_x4
ALU = mybir.AluOpType
ACT = mybir.ActivationFunctionType

P = 128
PACK = 4
K_PASS = P * PACK
TOKENS = 4 * 1024
D = 1024
F = 128
PASSES = D // K_PASS
BANK = 512
BANKS = 8
HALVES = D // BANK
BLOCKS = D // P
TILES = TOKENS // P
RUN = 4
PAIR = 2
PAIRS = TILES // PAIR
STEPS = 9
AHEAD = 2
EPS = 1e-5

FLOPS = 2 * TOKENS * D * D + 2 * TOKENS * D * F


def tile_flashinferblock_pb_t_kernel(
    tc, attn_out, x, w_proj, b_proj, g2, beta2, w_fc1, b_fc1, out_0, out_1
):
    nc = tc.nc
    attn_view = attn_out.flatten_outer_dims().rearrange("(p i) d -> p i d", i=TILES)
    x_view = x.flatten_outer_dims().rearrange("(p i) d -> p i d", i=TILES)
    x_mid_view = out_0.flatten_outer_dims().rearrange("(p i) d -> p i d", i=TILES)
    hid_view = out_1.flatten_outer_dims().rearrange("(p i) f -> p i f", i=TILES)

    with ExitStack() as ctx:
        const = ctx.enter_context(tc.tile_pool(name="const", bufs=1))
        loads = ctx.enter_context(tc.tile_pool(name="loads", bufs=AHEAD + 2))
        work = ctx.enter_context(tc.tile_pool(name="work", bufs=3))
        stats = ctx.enter_context(tc.tile_pool(name="stats", bufs=4))
        psum_const = ctx.enter_context(tc.psum_pool(name="psum_const", bufs=1))
        psum = ctx.enter_context(tc.psum_pool(name="psum", bufs=BANKS - HALVES))
        ctx.enter_context(tc.manual_schedule())

        attn_sb, x_sb, a_grouped, a_codes, a_scales, x_bias, x_mid = {}, {}, {}, {}, {}, {}, {}
        half_sums, neg_mean, inv_std, z, h_t, h_grouped, h_codes, h_scales, hid_biased = {}, {}, {}, {}, {}, {}, {}, {}, {}

        def bank(shape):
            return psum.tile(shape, F32, name="bank")

        def regroup(copy, grouped, planes):
            copy(
                out=grouped.rearrange("p (c i) t -> p c t i", i=RUN),
                in_=planes.rearrange("p t (c i) -> p c t i", i=RUN),
            )

        def tiles_of(pair):
            return slice(pair * PAIR, (pair + 1) * PAIR)

        def load(pair):
            attn_sb[pair] = loads.tile([P, PAIR, D], BF16, name="attn_sb")
            nc.sync.dma_start(out=attn_sb[pair][:], in_=attn_view[:, tiles_of(pair), :])
            x_sb[pair] = loads.tile([P, PAIR, D], BF16, name="x_sb")
            nc.sync.dma_start(out=x_sb[pair][:], in_=x_view[:, tiles_of(pair), :])

        w_raw = const.tile([P, PASSES, PACK, D], BF16)
        for g in range(PASSES):
            rows = w_proj[g * K_PASS : (g + 1) * K_PASS, :]
            nc.sync.dma_start(
                out=w_raw[:, g, :, :].rearrange("q (w e) c -> q w (e c)", e=2),
                in_=rows.rearrange("(w q e) c -> q w (e c)", w=2, e=2),
            )
        for pair in range(AHEAD):
            load(pair)

        norm_rows = const.tile([P, P], BF16)
        nc.vector.memset(norm_rows[:], 0.0)
        b_proj_row = const.tile([P, D], BF16)
        nc.vector.memset(b_proj_row[:], 0.0)
        ones = const.tile([P, P], BF16)
        nc.vector.memset(ones[:], 1.0)
        nc.scalar.dma_start(out=b_proj_row[0:1, :], in_=b_proj.rearrange("(o d) -> o d", o=1))
        nc.scalar.dma_start(out=norm_rows[0:BLOCKS, :], in_=g2.rearrange("(c p) -> c p", p=P))
        nc.scalar.dma_start(out=norm_rows[BLOCKS : 2 * BLOCKS, :], in_=beta2.rearrange("(c p) -> c p", p=P))
        f_raw = const.tile([P, PASSES, PACK, F], BF16)
        for g in range(PASSES):
            rows = w_fc1[g * K_PASS : (g + 1) * K_PASS, :]
            nc.scalar.dma_start(out=f_raw[:, g, :, :], in_=rows.rearrange("(t p) n -> p t n", p=P))
        b_fc1_all = const.tile([P, F], BF16)
        nc.scalar.dma_start(out=b_fc1_all[:], in_=b_fc1.partition_broadcast(P))

        ident = const.tile([P, P], F32)
        make_identity(nc, ident[:])
        neg_half = const.tile([P, PAIR], F32)
        nc.vector.memset(neg_half[:], -0.5)

        w_grouped = const.tile([P, PASSES, D, PACK], BF16, align_bytes=64)
        w_codes = const.tile([P, PASSES, D], U32, align_bytes=64)
        w_scales = const.tile([P, PASSES, D], U8, align_bytes=64)

        def regroup_w(g):
            for half in range(HALVES):
                cols = slice(half * BANK, (half + 1) * BANK)
                copy = nc.vector.tensor_copy if half == 0 else nc.scalar.copy
                regroup(copy, w_grouped[:, g, cols, :], w_raw[:, g, :, cols])

        regroup_w(0)

        b_proj_all = []
        for half in range(HALVES):
            b_proj_all.append(psum_const.tile([P, BANK], F32, name="b_proj_all%d" % half))
            nc.tensor.matmul(
                out=b_proj_all[half][:],
                lhsT=ones[:],
                rhs=b_proj_row[:, half * BANK : (half + 1) * BANK],
                start=True,
                stop=True,
            )

        norm_rows_f32 = const.tile([P, P], F32)
        nc.vector.tensor_copy(out=norm_rows_f32[:], in_=norm_rows[:])
        norm_cols_ps = bank([P, BANK])
        nc.tensor.transpose(norm_cols_ps[:, 0:P], norm_rows_f32[:], ident[:])
        gain = const.tile([P, BLOCKS], F32)
        nc.vector.tensor_copy(out=gain[:], in_=norm_cols_ps[:, 0:BLOCKS])
        shift = const.tile([P, BLOCKS], F32)
        nc.vector.tensor_copy(out=shift[:], in_=norm_cols_ps[:, BLOCKS : 2 * BLOCKS])

        f_grouped = const.tile([P, PASSES, F, PACK], BF16, align_bytes=64)
        for g in range(PASSES):
            regroup(nc.vector.tensor_copy, f_grouped[:, g, :, :], f_raw[:, g, :, :])
        f_codes = const.tile([P, PASSES, F], U32, align_bytes=64)
        f_scales = const.tile([P, PASSES, F], U8, align_bytes=64)

        regroup_w(1)
        nc.vector.quantize_mx(
            out=f_codes[:].rearrange("p g n -> p (g n)").bitcast(FP8X4),
            scales=f_scales[:].rearrange("p g n -> p (g n)"),
            in_=f_grouped[:].rearrange("p g n t -> p (g n t)"),
        )
        for half in range(HALVES):
            for g in range(PASSES):
                cols = slice(half * BANK, (half + 1) * BANK)
                nc.vector.quantize_mx(
                    out=w_codes[:, g, cols].bitcast(FP8X4),
                    scales=w_scales[:, g, cols],
                    in_=w_grouped[:, g, cols, :].rearrange("p c t -> p (c t)"),
                )

        def transpose_attn(pair):
            a_grouped[pair] = work.tile([P, PASSES, PAIR, P, PACK], BF16, name="a_grouped", align_bytes=64)
            a_words = a_grouped[pair][:].bitcast(F32)
            for j in range(PAIR):
                attn_words = attn_sb[pair][:, j, :].bitcast(F32)
                attn_t = bank([P, PASSES * 2, P])
                for c in range(PASSES * 2):
                    nc.tensor.transpose(attn_t[:, c, :], attn_words[:, c * P : (c + 1) * P], ident[:])
                nc.scalar.copy(out=a_words[:, :, j, :, :], in_=attn_t[:].rearrange("p (g w) r -> p g r w", w=2))

        def quantise_attn(pair):
            a_codes[pair] = work.tile([P, PASSES, PAIR, P], U32, name="a_codes", align_bytes=64)
            a_scales[pair] = work.tile([P, PASSES, PAIR, P], U8, name="a_scales", align_bytes=64)
            nc.vector.quantize_mx(
                out=a_codes[pair][:].rearrange("p g j r -> p (g j r)").bitcast(FP8X4),
                scales=a_scales[pair][:].rearrange("p g j r -> p (g j r)"),
                in_=a_grouped[pair][:].rearrange("p g j r t -> p (g j r t)"),
            )

        def add_bias(pair):
            x_bias[pair] = work.tile([P, PAIR, D], F32, name="x_bias", bufs=2)
            for half in range(HALVES):
                cols = slice(half * BANK, (half + 1) * BANK)
                nc.vector.tensor_tensor(
                    out=x_bias[pair][:, :, cols],
                    in0=b_proj_all[half][:].unsqueeze(1).to_broadcast([P, PAIR, BANK]),
                    in1=x_sb[pair][:, :, cols],
                    op=ALU.add,
                )

        def project(pair):
            x_mid[pair] = work.tile([P, PAIR, D], F32, name="x_mid", bufs=4)
            half_sums[pair] = stats.tile([P, PAIR, HALVES], F32, name="half_sums")
            for j in range(PAIR):
                for half in range(HALVES):
                    cols = slice(half * BANK, (half + 1) * BANK)
                    acc = bank([P, BANK])
                    for g in range(PASSES):
                        nc.tensor.matmul_mx(
                            out=acc[:],
                            lhsT=a_codes[pair][:, g, j, :].bitcast(FP8X4),
                            lhsT_scale=a_scales[pair][:, g, j, :],
                            rhs=w_codes[:, g, cols].bitcast(FP8X4),
                            rhs_scale=w_scales[:, g, cols],
                            start=(g == 0),
                            stop=(g == PASSES - 1),
                        )
                    nc.vector.scalar_tensor_tensor(
                        out=x_mid[pair][:, j, cols],
                        in0=acc[:],
                        scalar=1.0,
                        in1=x_bias[pair][:, j, cols],
                        op0=ALU.mult,
                        op1=ALU.add,
                        accum_out=half_sums[pair][:, j, half : half + 1],
                    )
            nc.sync.dma_start(out=x_mid_view[:, tiles_of(pair), :], in_=x_mid[pair][:])

        def variance(pair):
            neg_mean[pair] = stats.tile([P, PAIR], F32, name="neg_mean")
            sum_squares = stats.tile([P, PAIR], F32)
            for j in range(PAIR):
                scaled_sums = stats.tile([P, HALVES], F32)
                nc.scalar.activation(
                    out=scaled_sums[:],
                    in_=half_sums[pair][:, j, :],
                    func=ACT.Copy,
                    scale=-1.0 / D,
                    accum_out=neg_mean[pair][:, j : j + 1],
                )
                squares = work.tile([P, D], BF16, bufs=1)
                nc.scalar.activation(
                    out=squares[:],
                    in_=x_mid[pair][:, j, :],
                    func=ACT.Square,
                    bias=neg_mean[pair][:, j : j + 1],
                    scale=1.0,
                    accum_out=sum_squares[:, j : j + 1],
                )
            var_eps = stats.tile([P, PAIR], F32)
            nc.gpsimd.tensor_scalar(
                out=var_eps[:], in0=sum_squares[:], scalar1=1.0 / D, scalar2=EPS, op0=ALU.mult, op1=ALU.add
            )
            inv_std[pair] = stats.tile([P, PAIR], F32, name="inv_std")
            nc.gpsimd.tensor_tensor(out=inv_std[pair][:], in0=var_eps[:], in1=neg_half[:], op=ALU.pow)

        def normalise(pair):
            z[pair] = work.tile([P, PAIR, D], F32, name="z")
            for j in range(PAIR):
                nc.gpsimd.tensor_scalar(
                    out=z[pair][:, j, :],
                    in0=x_mid[pair][:, j, :],
                    scalar1=neg_mean[pair][:, j : j + 1],
                    scalar2=inv_std[pair][:, j : j + 1],
                    op0=ALU.add,
                    op1=ALU.mult,
                )

        def regroup_h(copy, pair, g, tokens):
            planes = h_t[pair][:, g * PACK : (g + 1) * PACK, :, :].rearrange("p t j r -> p t (j r)")
            regroup(copy, h_grouped[pair][:, g, tokens, :], planes[:, :, tokens])

        def regroup_h_vector(pair):
            regroup_h(nc.vector.tensor_copy, pair, 0, slice(0, PAIR * P))
            regroup_h(nc.vector.tensor_copy, pair, 1, slice(0, P))

        def transpose_norm(pair):
            h_t[pair] = work.tile([P, BLOCKS, PAIR, P], BF16, name="h_t")
            h_grouped[pair] = work.tile([P, PASSES, PAIR * P, PACK], BF16, name="h_grouped", align_bytes=64)
            for first in range(0, BLOCKS, 2):
                z_t = bank([P, 2, PAIR, P])
                for c in range(first, first + 2):
                    for j in range(PAIR):
                        nc.tensor.transpose(z_t[:, c - first, j, :], z[pair][:, j, c * P : (c + 1) * P], ident[:])
                for c in range(first, first + 2):
                    nc.scalar.activation(
                        out=h_t[pair][:, c, :, :],
                        in_=z_t[:, c - first, :, :],
                        func=ACT.Identity,
                        scale=gain[:, c : c + 1],
                        bias=shift[:, c : c + 1],
                    )
            regroup_h(nc.scalar.copy, pair, 1, slice(P, PAIR * P))

        def quantise_h(pair):
            h_codes[pair] = work.tile([P, PASSES, PAIR, P], U32, name="h_codes", align_bytes=64)
            h_scales[pair] = work.tile([P, PASSES, PAIR, P], U8, name="h_scales", align_bytes=64)
            nc.vector.quantize_mx(
                out=h_codes[pair][:].rearrange("p g j r -> p (g j r)").bitcast(FP8X4),
                scales=h_scales[pair][:].rearrange("p g j r -> p (g j r)"),
                in_=h_grouped[pair][:].rearrange("p g r t -> p (g r t)"),
            )

        def second_product(pair):
            hid_ps = bank([P, PAIR, F])
            for j in range(PAIR):
                for g in range(PASSES):
                    nc.tensor.matmul_mx(
                        out=hid_ps[:, j, :],
                        lhsT=h_codes[pair][:, g, j, :].bitcast(FP8X4),
                        lhsT_scale=h_scales[pair][:, g, j, :],
                        rhs=f_codes[:, g, :].bitcast(FP8X4),
                        rhs_scale=f_scales[:, g, :],
                        start=(g == 0),
                        stop=(g == PASSES - 1),
                    )
            hid_biased[pair] = work.tile([P, PAIR, F], F32, name="hid_biased")
            nc.vector.tensor_tensor(
                out=hid_biased[pair][:],
                in0=hid_ps[:],
                in1=b_fc1_all[:].unsqueeze(1).to_broadcast([P, PAIR, F]),
                op=ALU.add,
            )

        def finish(pair):
            hid_sb = work.tile([P, PAIR, F], F32)
            nc.scalar.activation(out=hid_sb[:], in_=hid_biased[pair][:], func=ACT.Gelu)
            nc.sync.dma_start(out=hid_view[:, tiles_of(pair), :], in_=hid_sb[:])

        def step(function, pair):
            if 0 <= pair < PAIRS:
                function(pair)

        for m in range(PAIRS + STEPS - 1):
            step(load, m + AHEAD)
            step(project, m - 2)
            step(finish, m - 8)
            step(variance, m - 3)
            step(normalise, m - 3)
            step(regroup_h_vector, m - 6)
            step(quantise_attn, m - 1)
            step(transpose_norm, m - 5)
            step(quantise_h, m - 6)
            step(add_bias, m - 1)
            step(transpose_attn, m)
            step(second_product, m - 7)
